import numpy as np
import ml_dtypes

BF16 = ml_dtypes.bfloat16


def bf(x):
    return np.asarray(x, np.float32).astype(BF16)


def f32(x):
    return np.asarray(x, np.float32)


def f64(x):
    return np.asarray(x).astype(np.float64)


def striped(idx):
    return np.tile(idx.reshape(-1, 16).T, (8, 1))


C, S, N, T, Q, E = 512, 1024, 2048, 16, 128, 256


def setup_inputs():
    x = f32(np.random.standard_normal((C, S)))
    mask = f32(np.tile((0.5 + np.random.random((1, N))) / np.sqrt(T), (C, 1)))
    w = bf(np.random.standard_normal((C, E)) / np.sqrt(C))
    b = f32(0.1 * np.random.standard_normal((E, 1)))
    offs = striped(np.random.permutation(np.tile(np.arange(S), 2))[:N])
    return {"x": x, "mask": mask, "w": w, "b": b, "offs": offs}


def reference(x, mask, w, b, offs):
    idx = offs[:16].T.reshape(-1)
    picked = f64(x)[:, idx] * f64(mask)
    pooled = picked.reshape(C, Q, T).sum(axis=2)
    return np.tanh(f64(w).T @ pooled + f64(b))

@@ -1,0 +1,81 @@
+import concourse.mybir as mybir
+
+F32, BF16, U16 = mybir.dt.float32, mybir.dt.bfloat16, mybir.dt.uint16
+
+P = 128
+C, S, N, T, Q, E = 512, 1024, 2048, 16, 128, 256
+C_BLOCKS = C // P
+E_BLOCKS = E // P
+PIECE = S
+PIECES = N // PIECE
+PIECE_Q = PIECE // T
+
+FLOPS = 2 * C * N + 2 * C * E * Q
+BYTES = 4 * C * S + 4 * N + 2 * C * E + 4 * E + 2 * P * (N // 16) + 4 * E * Q
+
+
+def tile_graphstatelstm_kernel(tc, x, mask, w, b, offs, out):
+    nc = tc.nc
+    with (
+        tc.tile_pool(name="held", bufs=1) as held,
+        tc.tile_pool(name="windows", bufs=C_BLOCKS) as windows,
+        tc.tile_pool(name="products", bufs=2) as products,
+        tc.tile_pool(name="results", bufs=E_BLOCKS) as results,
+        tc.psum_pool(name="psum", bufs=1) as psum,
+    ):
+        offsets = held.tile([P, N // 16], U16, name="offsets")
+        nc.sync.dma_start(offsets[:], offs)
+
+        weights_of_entries = held.tile([P, N], F32, name="weights_of_entries")
+        nc.scalar.dma_start(weights_of_entries[:], mask[0:P, :])
+
+        x_blocks = []
+        for cb in range(C_BLOCKS):
+            x_block = windows.tile([P, S], F32, name="x_block")
+            nc.sync.dma_start(x_block[:], x[cb * P : (cb + 1) * P, :])
+            x_blocks.append(x_block)
+
+        w_blocks = held.tile([P, C_BLOCKS, E], BF16, name="w_blocks")
+        nc.scalar.dma_start(w_blocks[:], w.rearrange("(cb p) e -> p cb e", p=P))
+        biases = []
+        for eb in range(E_BLOCKS):
+            bias = held.tile([P, 1], F32, name=f"bias{eb}")
+            nc.scalar.dma_start(bias[:], b[eb * P : (eb + 1) * P, :])
+            biases.append(bias)
+
+        pooled = held.tile([P, C_BLOCKS, Q], BF16, name="pooled")
+        sums = [psum.tile([P, Q], F32, name=f"sums{eb}") for eb in range(E_BLOCKS)]
+
+        for cb in range(C_BLOCKS):
+            for piece in range(PIECES):
+                product = products.tile([P, PIECE], F32, name="product")
+                nc.vector.tensor_tensor(
+                    product[:],
+                    x_blocks[cb][:].indirect(
+                        offsets[:, piece * (PIECE // 16) : (piece + 1) * (PIECE // 16)]
+                    ),
+                    weights_of_entries[:, piece * PIECE : (piece + 1) * PIECE],
+                    mybir.AluOpType.mult,
+                )
+                with nc.allow_low_precision(reason="pooled is rounded once to bfloat16"):
+                    nc.vector.tensor_reduce(
+                        pooled[:, cb, piece * PIECE_Q : (piece + 1) * PIECE_Q],
+                        product[:].rearrange("p (m t) -> p m t", t=T),
+                        mybir.AxisListType.X,
+                        mybir.AluOpType.add,
+                    )
+            for eb in range(E_BLOCKS):
+                nc.tensor.matmul(
+                    sums[eb][:],
+                    w_blocks[:, cb, eb * P : (eb + 1) * P],
+                    pooled[:, cb, :],
+                    start=(cb == 0),
+                    stop=(cb == C_BLOCKS - 1),
+                )
+
+        for eb in range(E_BLOCKS):
+            result = results.tile([P, Q], F32, name="result")
+            nc.scalar.activation(
+                result[:], sums[eb][:], mybir.ActivationFunctionType.Tanh, bias=biases[eb][:]
+            )
+            nc.sync.dma_start(out[eb * P : (eb + 1) * P, :], result[:])

@@ -1,4 +1,5 @@
 import concourse.mybir as mybir
+from concourse.masks import make_identity
 
 F32, BF16, U16 = mybir.dt.float32, mybir.dt.bfloat16, mybir.dt.uint16
 
@@ -19,9 +20,10 @@ def tile_graphstatelstm_kernel(tc, x, mask, w, b, offs, out):
     with (
         tc.tile_pool(name="held", bufs=1) as held,
         tc.tile_pool(name="windows", bufs=C_BLOCKS) as windows,
-        tc.tile_pool(name="products", bufs=2) as products,
+        tc.tile_pool(name="products", bufs=3) as products,
         tc.tile_pool(name="results", bufs=E_BLOCKS) as results,
         tc.psum_pool(name="psum", bufs=1) as psum,
+        tc.psum_pool(name="psum_pooled", bufs=2) as psum_pooled,
     ):
         offsets = held.tile([P, N // 16], U16, name="offsets")
         nc.sync.dma_start(offsets[:], offs)
@@ -43,6 +45,9 @@ def tile_graphstatelstm_kernel(tc, x, mask, w, b, offs, out):
             nc.scalar.dma_start(bias[:], b[eb * P : (eb + 1) * P, :])
             biases.append(bias)
 
+        identity = held.tile([P, P], F32, name="identity")
+        make_identity(nc, identity[:])
+
         pooled = held.tile([P, C_BLOCKS, Q], BF16, name="pooled")
         sums = [psum.tile([P, Q], F32, name=f"sums{eb}") for eb in range(E_BLOCKS)]
 
@@ -57,13 +62,17 @@ def tile_graphstatelstm_kernel(tc, x, mask, w, b, offs, out):
                     weights_of_entries[:, piece * PIECE : (piece + 1) * PIECE],
                     mybir.AluOpType.mult,
                 )
-                with nc.allow_low_precision(reason="pooled is rounded once to bfloat16"):
-                    nc.vector.tensor_reduce(
-                        pooled[:, cb, piece * PIECE_Q : (piece + 1) * PIECE_Q],
-                        product[:].rearrange("p (m t) -> p m t", t=T),
-                        mybir.AxisListType.X,
-                        mybir.AluOpType.add,
+                by_token = product[:].rearrange("p (m t) -> p t m", t=T)
+                pooled_f32 = psum_pooled.tile([P, PIECE_Q], F32, name="pooled_f32")
+                for t in range(T):
+                    nc.tensor.matmul(
+                        pooled_f32[:], identity[:], by_token[:, t, :], start=(t == 0), stop=(t == T - 1)
                     )
+                nc.scalar.activation(
+                    pooled[:, cb, piece * PIECE_Q : (piece + 1) * PIECE_Q],
+                    pooled_f32[:],
+                    mybir.ActivationFunctionType.Copy,
+                )
             for eb in range(E_BLOCKS):
                 nc.tensor.matmul(
                     sums[eb][:],

@@ -10,6 +10,7 @@ E_BLOCKS = E // P
 PIECE = S
 PIECES = N // PIECE
 PIECE_Q = PIECE // T
+GPSIMD_HALVINGS = 2
 
 FLOPS = 2 * C * N + 2 * C * E * Q
 BYTES = 4 * C * S + 4 * N + 2 * C * E + 4 * E + 2 * P * (N // 16) + 4 * E * Q
@@ -21,6 +22,7 @@ def tile_graphstatelstm_kernel(tc, x, mask, w, b, offs, out):
         tc.tile_pool(name="held", bufs=1) as held,
         tc.tile_pool(name="windows", bufs=C_BLOCKS) as windows,
         tc.tile_pool(name="products", bufs=3) as products,
+        tc.tile_pool(name="halves", bufs=2) as halves,
         tc.tile_pool(name="results", bufs=E_BLOCKS) as results,
         tc.psum_pool(name="psum", bufs=1) as psum,
         tc.psum_pool(name="psum_pooled", bufs=2) as psum_pooled,
@@ -62,11 +64,22 @@ def tile_graphstatelstm_kernel(tc, x, mask, w, b, offs, out):
                     weights_of_entries[:, piece * PIECE : (piece + 1) * PIECE],
                     mybir.AluOpType.mult,
                 )
-                by_token = product[:].rearrange("p (m t) -> p t m", t=T)
+                terms = product[:].rearrange("p (m t) -> p m t", t=T)
+                n_terms = T
+                for halving in range(GPSIMD_HALVINGS):
+                    n_terms //= 2
+                    halved = halves.tile([P, PIECE_Q, n_terms], F32, name=f"halved{n_terms}")
+                    nc.gpsimd.tensor_tensor(
+                        halved[:],
+                        terms[:, :, 0:n_terms],
+                        terms[:, :, n_terms : 2 * n_terms],
+                        mybir.AluOpType.add,
+                    )
+                    terms = halved
                 pooled_f32 = psum_pooled.tile([P, PIECE_Q], F32, name="pooled_f32")
-                for t in range(T):
+                for t in range(n_terms):
                     nc.tensor.matmul(
-                        pooled_f32[:], identity[:], by_token[:, t, :], start=(t == 0), stop=(t == T - 1)
+                        pooled_f32[:], identity[:], terms[:, :, t], start=(t == 0), stop=(t == n_terms - 1)
                     )
                 nc.scalar.activation(
                     pooled[:, cb, piece * PIECE_Q : (piece + 1) * PIECE_Q],

@@ -10,7 +10,6 @@ E_BLOCKS = E // P
 PIECE = S
 PIECES = N // PIECE
 PIECE_Q = PIECE // T
-GPSIMD_HALVINGS = 2
 
 FLOPS = 2 * C * N + 2 * C * E * Q
 BYTES = 4 * C * S + 4 * N + 2 * C * E + 4 * E + 2 * P * (N // 16) + 4 * E * Q
@@ -18,14 +17,13 @@ BYTES = 4 * C * S + 4 * N + 2 * C * E + 4 * E + 2 * P * (N // 16) + 4 * E * Q
 
 def tile_graphstatelstm_kernel(tc, x, mask, w, b, offs, out):
     nc = tc.nc
+    mult, add = mybir.AluOpType.mult, mybir.AluOpType.add
     with (
         tc.tile_pool(name="held", bufs=1) as held,
         tc.tile_pool(name="windows", bufs=C_BLOCKS) as windows,
-        tc.tile_pool(name="products", bufs=3) as products,
-        tc.tile_pool(name="halves", bufs=2) as halves,
-        tc.tile_pool(name="results", bufs=E_BLOCKS) as results,
+        tc.tile_pool(name="products", bufs=2) as products,
+        tc.tile_pool(name="results", bufs=PIECES * E_BLOCKS) as results,
         tc.psum_pool(name="psum", bufs=1) as psum,
-        tc.psum_pool(name="psum_pooled", bufs=2) as psum_pooled,
     ):
         offsets = held.tile([P, N // 16], U16, name="offsets")
         nc.sync.dma_start(offsets[:], offs)
@@ -50,42 +48,17 @@ def tile_graphstatelstm_kernel(tc, x, mask, w, b, offs, out):
         identity = held.tile([P, P], F32, name="identity")
         make_identity(nc, identity[:])
 
-        pooled = held.tile([P, C_BLOCKS, Q], BF16, name="pooled")
-        sums = [psum.tile([P, Q], F32, name=f"sums{eb}") for eb in range(E_BLOCKS)]
+        def gather_times_mask(product, cb, piece):
+            nc.vector.tensor_tensor(
+                product,
+                x_blocks[cb][:].indirect(
+                    offsets[:, piece * (PIECE // 16) : (piece + 1) * (PIECE // 16)]
+                ),
+                weights_of_entries[:, piece * PIECE : (piece + 1) * PIECE],
+                mult,
+            )
 
-        for cb in range(C_BLOCKS):
-            for piece in range(PIECES):
-                product = products.tile([P, PIECE], F32, name="product")
-                nc.vector.tensor_tensor(
-                    product[:],
-                    x_blocks[cb][:].indirect(
-                        offsets[:, piece * (PIECE // 16) : (piece + 1) * (PIECE // 16)]
-                    ),
-                    weights_of_entries[:, piece * PIECE : (piece + 1) * PIECE],
-                    mybir.AluOpType.mult,
-                )
-                terms = product[:].rearrange("p (m t) -> p m t", t=T)
-                n_terms = T
-                for halving in range(GPSIMD_HALVINGS):
-                    n_terms //= 2
-                    halved = halves.tile([P, PIECE_Q, n_terms], F32, name=f"halved{n_terms}")
-                    nc.gpsimd.tensor_tensor(
-                        halved[:],
-                        terms[:, :, 0:n_terms],
-                        terms[:, :, n_terms : 2 * n_terms],
-                        mybir.AluOpType.add,
-                    )
-                    terms = halved
-                pooled_f32 = psum_pooled.tile([P, PIECE_Q], F32, name="pooled_f32")
-                for t in range(n_terms):
-                    nc.tensor.matmul(
-                        pooled_f32[:], identity[:], terms[:, :, t], start=(t == 0), stop=(t == n_terms - 1)
-                    )
-                nc.scalar.activation(
-                    pooled[:, cb, piece * PIECE_Q : (piece + 1) * PIECE_Q],
-                    pooled_f32[:],
-                    mybir.ActivationFunctionType.Copy,
-                )
+        def linear_block(sums, pooled, cb):
             for eb in range(E_BLOCKS):
                 nc.tensor.matmul(
                     sums[eb][:],
@@ -95,9 +68,48 @@ def tile_graphstatelstm_kernel(tc, x, mask, w, b, offs, out):
                     stop=(cb == C_BLOCKS - 1),
                 )
 
-        for eb in range(E_BLOCKS):
-            result = results.tile([P, Q], F32, name="result")
-            nc.scalar.activation(
-                result[:], sums[eb][:], mybir.ActivationFunctionType.Tanh, bias=biases[eb][:]
+        def tanh_and_store(sums, piece):
+            for eb in range(E_BLOCKS):
+                result = results.tile([P, PIECE_Q], F32, name="result")
+                nc.scalar.activation(
+                    result[:], sums[eb][:], mybir.ActivationFunctionType.Tanh, bias=biases[eb][:]
+                )
+                nc.sync.dma_start(
+                    out[eb * P : (eb + 1) * P, piece * PIECE_Q : (piece + 1) * PIECE_Q], result[:]
+                )
+
+
+        products0 = held.tile([P, C_BLOCKS * PIECE], F32, name="products0")
+        for cb in range(C_BLOCKS):
+            gather_times_mask(products0[:, cb * PIECE : (cb + 1) * PIECE], cb, 0)
+        by_token = products0[:].rearrange("p (cb_m t) -> p t cb_m", t=T)
+        pooled0_f32 = psum.tile([P, C_BLOCKS * PIECE_Q], F32, name="pooled0_f32")
+        for t in range(T):
+            nc.tensor.matmul(
+                pooled0_f32[:], identity[:], by_token[:, t, :], start=(t == 0), stop=(t == T - 1)
             )
-            nc.sync.dma_start(out[eb * P : (eb + 1) * P, :], result[:])
+        pooled0 = held.tile([P, C_BLOCKS, PIECE_Q], BF16, name="pooled0")
+        nc.scalar.activation(
+            pooled0[:].rearrange("p cb m -> p (cb m)"),
+            pooled0_f32[:],
+            mybir.ActivationFunctionType.Copy,
+        )
+        sums0 = [psum.tile([P, PIECE_Q], F32, name=f"sums0_{eb}") for eb in range(E_BLOCKS)]
+        for cb in range(C_BLOCKS):
+            linear_block(sums0, pooled0, cb)
+        tanh_and_store(sums0, 0)
+
+        pooled1 = held.tile([P, C_BLOCKS, PIECE_Q], BF16, name="pooled1")
+        sums1 = [psum.tile([P, PIECE_Q], F32, name=f"sums1_{eb}") for eb in range(E_BLOCKS)]
+        for cb in range(C_BLOCKS):
+            product = products.tile([P, PIECE], F32, name="product")
+            gather_times_mask(product[:], cb, 1)
+            with nc.allow_low_precision(reason="pooled is rounded once to bfloat16"):
+                nc.vector.tensor_reduce(
+                    pooled1[:, cb, :],
+                    product[:].rearrange("p (m t) -> p m t", t=T),
+                    mybir.AxisListType.X,
+                    add,
+                )
+            linear_block(sums1, pooled1, cb)
+        tanh_and_store(sums1, 1)

@@ -1,5 +1,4 @@
 import concourse.mybir as mybir
-from concourse.masks import make_identity
 
 F32, BF16, U16 = mybir.dt.float32, mybir.dt.bfloat16, mybir.dt.uint16
 
@@ -17,19 +16,21 @@ BYTES = 4 * C * S + 4 * N + 2 * C * E + 4 * E + 2 * P * (N // 16) + 4 * E * Q
 
 def tile_graphstatelstm_kernel(tc, x, mask, w, b, offs, out):
     nc = tc.nc
-    mult, add = mybir.AluOpType.mult, mybir.AluOpType.add
     with (
         tc.tile_pool(name="held", bufs=1) as held,
         tc.tile_pool(name="windows", bufs=C_BLOCKS) as windows,
         tc.tile_pool(name="products", bufs=2) as products,
-        tc.tile_pool(name="results", bufs=PIECES * E_BLOCKS) as results,
+        tc.tile_pool(name="results", bufs=E_BLOCKS) as results,
         tc.psum_pool(name="psum", bufs=1) as psum,
     ):
         offsets = held.tile([P, N // 16], U16, name="offsets")
         nc.sync.dma_start(offsets[:], offs)
 
-        weights_of_entries = held.tile([P, N], F32, name="weights_of_entries")
-        nc.scalar.dma_start(weights_of_entries[:], mask[0:P, :])
+        entry_weights = []
+        for piece in range(PIECES):
+            piece_weights = held.tile([P, PIECE], F32, name=f"entry_weights{piece}")
+            nc.scalar.dma_start(piece_weights[:], mask[0:P, piece * PIECE : (piece + 1) * PIECE])
+            entry_weights.append(piece_weights)
 
         x_blocks = []
         for cb in range(C_BLOCKS):
@@ -45,20 +46,27 @@ def tile_graphstatelstm_kernel(tc, x, mask, w, b, offs, out):
             nc.scalar.dma_start(bias[:], b[eb * P : (eb + 1) * P, :])
             biases.append(bias)
 
-        identity = held.tile([P, P], F32, name="identity")
-        make_identity(nc, identity[:])
+        pooled = held.tile([P, C_BLOCKS, Q], BF16, name="pooled")
+        sums = [psum.tile([P, Q], F32, name=f"sums{eb}") for eb in range(E_BLOCKS)]
 
-        def gather_times_mask(product, cb, piece):
-            nc.vector.tensor_tensor(
-                product,
-                x_blocks[cb][:].indirect(
-                    offsets[:, piece * (PIECE // 16) : (piece + 1) * (PIECE // 16)]
-                ),
-                weights_of_entries[:, piece * PIECE : (piece + 1) * PIECE],
-                mult,
-            )
-
-        def linear_block(sums, pooled, cb):
+        for cb in range(C_BLOCKS):
+            for piece in range(PIECES):
+                product = products.tile([P, PIECE], F32, name="product")
+                nc.vector.tensor_tensor(
+                    product[:],
+                    x_blocks[cb][:].indirect(
+                        offsets[:, piece * (PIECE // 16) : (piece + 1) * (PIECE // 16)]
+                    ),
+                    entry_weights[piece][:],
+                    mybir.AluOpType.mult,
+                )
+                with nc.allow_low_precision(reason="pooled is rounded once to bfloat16"):
+                    nc.vector.tensor_reduce(
+                        pooled[:, cb, piece * PIECE_Q : (piece + 1) * PIECE_Q],
+                        product[:].rearrange("p (m t) -> p m t", t=T),
+                        mybir.AxisListType.X,
+                        mybir.AluOpType.add,
+                    )
             for eb in range(E_BLOCKS):
                 nc.tensor.matmul(
                     sums[eb][:],
@@ -68,48 +76,9 @@ def tile_graphstatelstm_kernel(tc, x, mask, w, b, offs, out):
                     stop=(cb == C_BLOCKS - 1),
                 )
 
-        def tanh_and_store(sums, piece):
-            for eb in range(E_BLOCKS):
-                result = results.tile([P, PIECE_Q], F32, name="result")
-                nc.scalar.activation(
-                    result[:], sums[eb][:], mybir.ActivationFunctionType.Tanh, bias=biases[eb][:]
-                )
-                nc.sync.dma_start(
-                    out[eb * P : (eb + 1) * P, piece * PIECE_Q : (piece + 1) * PIECE_Q], result[:]
-                )
-
-
-        products0 = held.tile([P, C_BLOCKS * PIECE], F32, name="products0")
-        for cb in range(C_BLOCKS):
-            gather_times_mask(products0[:, cb * PIECE : (cb + 1) * PIECE], cb, 0)
-        by_token = products0[:].rearrange("p (cb_m t) -> p t cb_m", t=T)
-        pooled0_f32 = psum.tile([P, C_BLOCKS * PIECE_Q], F32, name="pooled0_f32")
-        for t in range(T):
-            nc.tensor.matmul(
-                pooled0_f32[:], identity[:], by_token[:, t, :], start=(t == 0), stop=(t == T - 1)
+        for eb in range(E_BLOCKS):
+            result = results.tile([P, Q], F32, name="result")
+            nc.scalar.activation(
+                result[:], sums[eb][:], mybir.ActivationFunctionType.Tanh, bias=biases[eb][:]
             )
-        pooled0 = held.tile([P, C_BLOCKS, PIECE_Q], BF16, name="pooled0")
-        nc.scalar.activation(
-            pooled0[:].rearrange("p cb m -> p (cb m)"),
-            pooled0_f32[:],
-            mybir.ActivationFunctionType.Copy,
-        )
-        sums0 = [psum.tile([P, PIECE_Q], F32, name=f"sums0_{eb}") for eb in range(E_BLOCKS)]
-        for cb in range(C_BLOCKS):
-            linear_block(sums0, pooled0, cb)
-        tanh_and_store(sums0, 0)
-
-        pooled1 = held.tile([P, C_BLOCKS, PIECE_Q], BF16, name="pooled1")
-        sums1 = [psum.tile([P, PIECE_Q], F32, name=f"sums1_{eb}") for eb in range(E_BLOCKS)]
-        for cb in range(C_BLOCKS):
-            product = products.tile([P, PIECE], F32, name="product")
-            gather_times_mask(product[:], cb, 1)
-            with nc.allow_low_precision(reason="pooled is rounded once to bfloat16"):
-                nc.vector.tensor_reduce(
-                    pooled1[:, cb, :],
-                    product[:].rearrange("p (m t) -> p m t", t=T),
-                    mybir.AxisListType.X,
-                    add,
-                )
-            linear_block(sums1, pooled1, cb)
-        tanh_and_store(sums1, 1)
+            nc.sync.dma_start(out[eb * P : (eb + 1) * P, :], result[:])

@@ -1,4 +1,5 @@
 import concourse.mybir as mybir
+from concourse.masks import make_identity
 
 F32, BF16, U16 = mybir.dt.float32, mybir.dt.bfloat16, mybir.dt.uint16
 
@@ -9,6 +10,8 @@ E_BLOCKS = E // P
 PIECE = S
 PIECES = N // PIECE
 PIECE_Q = PIECE // T
+TENSOR_Q = 48
+assert TENSOR_Q <= PIECE_Q
 
 FLOPS = 2 * C * N + 2 * C * E * Q
 BYTES = 4 * C * S + 4 * N + 2 * C * E + 4 * E + 2 * P * (N // 16) + 4 * E * Q
@@ -16,57 +19,72 @@ BYTES = 4 * C * S + 4 * N + 2 * C * E + 4 * E + 2 * P * (N // 16) + 4 * E * Q
 
 def tile_graphstatelstm_kernel(tc, x, mask, w, b, offs, out):
     nc = tc.nc
+    mult, add = mybir.AluOpType.mult, mybir.AluOpType.add
     with (
         tc.tile_pool(name="held", bufs=1) as held,
-        tc.tile_pool(name="windows", bufs=C_BLOCKS) as windows,
-        tc.tile_pool(name="products", bufs=2) as products,
+        tc.tile_pool(name="blocks", bufs=C_BLOCKS) as blocks,
         tc.tile_pool(name="results", bufs=E_BLOCKS) as results,
         tc.psum_pool(name="psum", bufs=1) as psum,
+        tc.psum_pool(name="psum_pooled", bufs=2) as psum_pooled,
     ):
         offsets = held.tile([P, N // 16], U16, name="offsets")
         nc.sync.dma_start(offsets[:], offs)
 
-        entry_weights = []
-        for piece in range(PIECES):
-            piece_weights = held.tile([P, PIECE], F32, name=f"entry_weights{piece}")
-            nc.scalar.dma_start(piece_weights[:], mask[0:P, piece * PIECE : (piece + 1) * PIECE])
-            entry_weights.append(piece_weights)
+        entry_weights = [
+            held.tile([P, PIECE], F32, name=f"entry_weights{piece}") for piece in range(PIECES)
+        ]
+        w_blocks = held.tile([P, C_BLOCKS, E], BF16, name="w_blocks")
+        biases = [held.tile([P, 1], F32, name=f"bias{eb}") for eb in range(E_BLOCKS)]
+        nc.scalar.dma_start(entry_weights[0][:], mask[0:P, 0:PIECE])
+        nc.scalar.dma_start(w_blocks[:], w.rearrange("(cb p) e -> p cb e", p=P))
+        for eb in range(E_BLOCKS):
+            nc.scalar.dma_start(biases[eb][:], b[eb * P : (eb + 1) * P, :])
+        nc.scalar.dma_start(entry_weights[1][:], mask[0:P, PIECE : 2 * PIECE])
 
         x_blocks = []
         for cb in range(C_BLOCKS):
-            x_block = windows.tile([P, S], F32, name="x_block")
+            x_block = blocks.tile([P, S], F32, name="x_block")
             nc.sync.dma_start(x_block[:], x[cb * P : (cb + 1) * P, :])
             x_blocks.append(x_block)
 
-        w_blocks = held.tile([P, C_BLOCKS, E], BF16, name="w_blocks")
-        nc.scalar.dma_start(w_blocks[:], w.rearrange("(cb p) e -> p cb e", p=P))
-        biases = []
-        for eb in range(E_BLOCKS):
-            bias = held.tile([P, 1], F32, name=f"bias{eb}")
-            nc.scalar.dma_start(bias[:], b[eb * P : (eb + 1) * P, :])
-            biases.append(bias)
+        identity = held.tile([P, P], F32, name="identity")
+        make_identity(nc, identity[:])
 
         pooled = held.tile([P, C_BLOCKS, Q], BF16, name="pooled")
         sums = [psum.tile([P, Q], F32, name=f"sums{eb}") for eb in range(E_BLOCKS)]
+        products = [blocks.tile([P, N], F32, name="product") for cb in range(C_BLOCKS)]
+
+        def gather_times_mask(cb, piece):
+            nc.vector.tensor_tensor(
+                products[cb][:, piece * PIECE : (piece + 1) * PIECE],
+                x_blocks[cb][:].indirect(
+                    offsets[:, piece * (PIECE // 16) : (piece + 1) * (PIECE // 16)]
+                ),
+                entry_weights[piece][:],
+                mult,
+            )
 
         for cb in range(C_BLOCKS):
-            for piece in range(PIECES):
-                product = products.tile([P, PIECE], F32, name="product")
-                nc.vector.tensor_tensor(
-                    product[:],
-                    x_blocks[cb][:].indirect(
-                        offsets[:, piece * (PIECE // 16) : (piece + 1) * (PIECE // 16)]
-                    ),
-                    entry_weights[piece][:],
-                    mybir.AluOpType.mult,
+            gather_times_mask(cb, 0)
+            by_token = products[cb][:, 0 : TENSOR_Q * T].rearrange("p (m t) -> p t m", t=T)
+            pooled_f32 = psum_pooled.tile([P, TENSOR_Q], F32, name="pooled_f32")
+            for t in range(T):
+                nc.tensor.matmul(
+                    pooled_f32[:], identity[:], by_token[:, t, :], start=(t == 0), stop=(t == T - 1)
                 )
-                with nc.allow_low_precision(reason="pooled is rounded once to bfloat16"):
-                    nc.vector.tensor_reduce(
-                        pooled[:, cb, piece * PIECE_Q : (piece + 1) * PIECE_Q],
-                        product[:].rearrange("p (m t) -> p m t", t=T),
-                        mybir.AxisListType.X,
-                        mybir.AluOpType.add,
-                    )
+            nc.scalar.activation(
+                pooled[:, cb, 0:TENSOR_Q], pooled_f32[:], mybir.ActivationFunctionType.Copy
+            )
+
+        for cb in range(C_BLOCKS):
+            gather_times_mask(cb, 1)
+            with nc.allow_low_precision(reason="pooled is rounded once to bfloat16"):
+                nc.vector.tensor_reduce(
+                    pooled[:, cb, TENSOR_Q:Q],
+                    products[cb][:, TENSOR_Q * T : N].rearrange("p (m t) -> p m t", t=T),
+                    mybir.AxisListType.X,
+                    add,
+                )
             for eb in range(E_BLOCKS):
                 nc.tensor.matmul(
                     sums[eb][:],

@@ -11,6 +11,7 @@ PIECE = S
 PIECES = N // PIECE
 PIECE_Q = PIECE // T
 TENSOR_Q = 48
+PAIR = 2
 assert TENSOR_Q <= PIECE_Q
 
 FLOPS = 2 * C * N + 2 * C * E * Q
@@ -52,11 +53,11 @@ def tile_graphstatelstm_kernel(tc, x, mask, w, b, offs, out):
 
         pooled = held.tile([P, C_BLOCKS, Q], BF16, name="pooled")
         sums = [psum.tile([P, Q], F32, name=f"sums{eb}") for eb in range(E_BLOCKS)]
-        products = [blocks.tile([P, N], F32, name="product") for cb in range(C_BLOCKS)]
+        products = [held.tile([P, PAIR, N], F32, name=f"products{pair}") for pair in range(C_BLOCKS // PAIR)]
 
         def gather_times_mask(cb, piece):
             nc.vector.tensor_tensor(
-                products[cb][:, piece * PIECE : (piece + 1) * PIECE],
+                products[cb // PAIR][:, cb % PAIR, piece * PIECE : (piece + 1) * PIECE],
                 x_blocks[cb][:].indirect(
                     offsets[:, piece * (PIECE // 16) : (piece + 1) * (PIECE // 16)]
                 ),
@@ -64,16 +65,19 @@ def tile_graphstatelstm_kernel(tc, x, mask, w, b, offs, out):
                 mult,
             )
 
-        for cb in range(C_BLOCKS):
-            gather_times_mask(cb, 0)
-            by_token = products[cb][:, 0 : TENSOR_Q * T].rearrange("p (m t) -> p t m", t=T)
-            pooled_f32 = psum_pooled.tile([P, TENSOR_Q], F32, name="pooled_f32")
+        for pair in range(C_BLOCKS // PAIR):
+            for cb in range(pair * PAIR, (pair + 1) * PAIR):
+                gather_times_mask(cb, 0)
+            by_token = products[pair][:, :, 0 : TENSOR_Q * T].rearrange("p k (m t) -> p t k m", t=T)
+            pooled_f32 = psum_pooled.tile([P, PAIR, TENSOR_Q], F32, name="pooled_f32")
             for t in range(T):
                 nc.tensor.matmul(
-                    pooled_f32[:], identity[:], by_token[:, t, :], start=(t == 0), stop=(t == T - 1)
+                    pooled_f32[:], identity[:], by_token[:, t], start=(t == 0), stop=(t == T - 1)
                 )
             nc.scalar.activation(
-                pooled[:, cb, 0:TENSOR_Q], pooled_f32[:], mybir.ActivationFunctionType.Copy
+                pooled[:, pair * PAIR : (pair + 1) * PAIR, 0:TENSOR_Q],
+                pooled_f32[:],
+                mybir.ActivationFunctionType.Copy,
             )
 
         for cb in range(C_BLOCKS):
@@ -81,7 +85,7 @@ def tile_graphstatelstm_kernel(tc, x, mask, w, b, offs, out):
             with nc.allow_low_precision(reason="pooled is rounded once to bfloat16"):
                 nc.vector.tensor_reduce(
                     pooled[:, cb, TENSOR_Q:Q],
-                    products[cb][:, TENSOR_Q * T : N].rearrange("p (m t) -> p m t", t=T),
+                    products[cb // PAIR][:, cb % PAIR, TENSOR_Q * T : N].rearrange("p (m t) -> p m t", t=T),
                     mybir.AxisListType.X,
                     add,
                 )

@@ -8,11 +8,11 @@ C, S, N, T, Q, E = 512, 1024, 2048, 16, 128, 256
 C_BLOCKS = C // P
 E_BLOCKS = E // P
 PIECE = S
-PIECES = N // PIECE
 PIECE_Q = PIECE // T
-TENSOR_Q = 48
 PAIR = 2
-assert TENSOR_Q <= PIECE_Q
+PAIRS = C_BLOCKS // PAIR
+BANK = 512
+WARM_UP_MATMULS = 12
 
 FLOPS = 2 * C * N + 2 * C * E * Q
 BYTES = 4 * C * S + 4 * N + 2 * C * E + 4 * E + 2 * P * (N // 16) + 4 * E * Q
@@ -23,17 +23,16 @@ def tile_graphstatelstm_kernel(tc, x, mask, w, b, offs, out):
     mult, add = mybir.AluOpType.mult, mybir.AluOpType.add
     with (
         tc.tile_pool(name="held", bufs=1) as held,
-        tc.tile_pool(name="blocks", bufs=C_BLOCKS) as blocks,
+        tc.tile_pool(name="windows", bufs=C_BLOCKS) as windows,
+        tc.tile_pool(name="products", bufs=2) as products,
         tc.tile_pool(name="results", bufs=E_BLOCKS) as results,
         tc.psum_pool(name="psum", bufs=1) as psum,
-        tc.psum_pool(name="psum_pooled", bufs=2) as psum_pooled,
+        tc.psum_pool(name="psum_pooled", bufs=PAIRS) as psum_pooled,
     ):
         offsets = held.tile([P, N // 16], U16, name="offsets")
         nc.sync.dma_start(offsets[:], offs)
 
-        entry_weights = [
-            held.tile([P, PIECE], F32, name=f"entry_weights{piece}") for piece in range(PIECES)
-        ]
+        entry_weights = [held.tile([P, PIECE], F32, name=f"entry_weights{piece}") for piece in range(2)]
         w_blocks = held.tile([P, C_BLOCKS, E], BF16, name="w_blocks")
         biases = [held.tile([P, 1], F32, name=f"bias{eb}") for eb in range(E_BLOCKS)]
         nc.scalar.dma_start(entry_weights[0][:], mask[0:P, 0:PIECE])
@@ -44,20 +43,16 @@ def tile_graphstatelstm_kernel(tc, x, mask, w, b, offs, out):
 
         x_blocks = []
         for cb in range(C_BLOCKS):
-            x_block = blocks.tile([P, S], F32, name="x_block")
+            x_block = windows.tile([P, S], F32, name="x_block")
             nc.sync.dma_start(x_block[:], x[cb * P : (cb + 1) * P, :])
             x_blocks.append(x_block)
 
         identity = held.tile([P, P], F32, name="identity")
         make_identity(nc, identity[:])
 
-        pooled = held.tile([P, C_BLOCKS, Q], BF16, name="pooled")
-        sums = [psum.tile([P, Q], F32, name=f"sums{eb}") for eb in range(E_BLOCKS)]
-        products = [held.tile([P, PAIR, N], F32, name=f"products{pair}") for pair in range(C_BLOCKS // PAIR)]
-
-        def gather_times_mask(cb, piece):
+        def gather_times_mask(product, cb, piece):
             nc.vector.tensor_tensor(
-                products[cb // PAIR][:, cb % PAIR, piece * PIECE : (piece + 1) * PIECE],
+                product,
                 x_blocks[cb][:].indirect(
                     offsets[:, piece * (PIECE // 16) : (piece + 1) * (PIECE // 16)]
                 ),
@@ -65,27 +60,46 @@ def tile_graphstatelstm_kernel(tc, x, mask, w, b, offs, out):
                 mult,
             )
 
-        for pair in range(C_BLOCKS // PAIR):
-            for cb in range(pair * PAIR, (pair + 1) * PAIR):
-                gather_times_mask(cb, 0)
-            by_token = products[pair][:, :, 0 : TENSOR_Q * T].rearrange("p k (m t) -> p t k m", t=T)
-            pooled_f32 = psum_pooled.tile([P, PAIR, TENSOR_Q], F32, name="pooled_f32")
+        warm_up = psum.tile([P, BANK], F32, name="warm_up")
+        for repeat in range(WARM_UP_MATMULS):
+            nc.tensor.matmul(
+                warm_up[:],
+                w_blocks[:, 0, 0:P],
+                w_blocks[:, 0 : BANK // E, :].rearrange("p cb e -> p (cb e)"),
+                start=True,
+                stop=True,
+            )
+
+        pooled = held.tile([P, C_BLOCKS, Q], BF16, name="pooled")
+
+        for pair in range(PAIRS):
+            pair_products = held.tile([P, PAIR, PIECE], F32, name=f"pair_products{pair}")
+            for k in range(PAIR):
+                gather_times_mask(pair_products[:, k, :], pair * PAIR + k, 0)
+            by_token = pair_products[:].rearrange("p k (m t) -> p t (k m)", t=T)
+            pooled_f32 = psum_pooled.tile([P, PAIR, PIECE_Q], F32, name="pooled_f32")
             for t in range(T):
                 nc.tensor.matmul(
-                    pooled_f32[:], identity[:], by_token[:, t], start=(t == 0), stop=(t == T - 1)
+                    pooled_f32[:].rearrange("p k m -> p (k m)"),
+                    identity[:],
+                    by_token[:, t, :],
+                    start=(t == 0),
+                    stop=(t == T - 1),
                 )
             nc.scalar.activation(
-                pooled[:, pair * PAIR : (pair + 1) * PAIR, 0:TENSOR_Q],
+                pooled[:, pair * PAIR : (pair + 1) * PAIR, 0:PIECE_Q],
                 pooled_f32[:],
                 mybir.ActivationFunctionType.Copy,
             )
 
+        sums = [psum.tile([P, Q], F32, name=f"sums{eb}") for eb in range(E_BLOCKS)]
         for cb in range(C_BLOCKS):
-            gather_times_mask(cb, 1)
+            product = products.tile([P, PIECE], F32, name="product")
+            gather_times_mask(product[:], cb, 1)
             with nc.allow_low_precision(reason="pooled is rounded once to bfloat16"):
                 nc.vector.tensor_reduce(
-                    pooled[:, cb, TENSOR_Q:Q],
-                    products[cb // PAIR][:, cb % PAIR, TENSOR_Q * T : N].rearrange("p (m t) -> p m t", t=T),
+                    pooled[:, cb, PIECE_Q:Q],
+                    product[:].rearrange("p (m t) -> p m t", t=T),
                     mybir.AxisListType.X,
                     add,
                 )

@@ -8,11 +8,7 @@ C, S, N, T, Q, E = 512, 1024, 2048, 16, 128, 256
 C_BLOCKS = C // P
 E_BLOCKS = E // P
 PIECE = S
-PIECE_Q = PIECE // T
-PAIR = 2
-PAIRS = C_BLOCKS // PAIR
-BANK = 512
-WARM_UP_MATMULS = 12
+PIECES = N // PIECE
 
 FLOPS = 2 * C * N + 2 * C * E * Q
 BYTES = 4 * C * S + 4 * N + 2 * C * E + 4 * E + 2 * P * (N // 16) + 4 * E * Q
@@ -21,88 +17,78 @@ BYTES = 4 * C * S + 4 * N + 2 * C * E + 4 * E + 2 * P * (N // 16) + 4 * E * Q
 def tile_graphstatelstm_kernel(tc, x, mask, w, b, offs, out):
     nc = tc.nc
     mult, add = mybir.AluOpType.mult, mybir.AluOpType.add
+    copy, tanh = mybir.ActivationFunctionType.Copy, mybir.ActivationFunctionType.Tanh
     with (
         tc.tile_pool(name="held", bufs=1) as held,
-        tc.tile_pool(name="windows", bufs=C_BLOCKS) as windows,
-        tc.tile_pool(name="products", bufs=2) as products,
+        tc.tile_pool(name="blocks", bufs=C_BLOCKS) as blocks,
         tc.tile_pool(name="results", bufs=E_BLOCKS) as results,
         tc.psum_pool(name="psum", bufs=1) as psum,
-        tc.psum_pool(name="psum_pooled", bufs=PAIRS) as psum_pooled,
+        tc.psum_pool(name="psum_blocks", bufs=2) as psum_blocks,
     ):
         offsets = held.tile([P, N // 16], U16, name="offsets")
         nc.sync.dma_start(offsets[:], offs)
 
-        entry_weights = [held.tile([P, PIECE], F32, name=f"entry_weights{piece}") for piece in range(2)]
+        entry_weights = [held.tile([P, PIECE], F32, name=f"entry_weights{piece}") for piece in range(PIECES)]
         w_blocks = held.tile([P, C_BLOCKS, E], BF16, name="w_blocks")
         biases = [held.tile([P, 1], F32, name=f"bias{eb}") for eb in range(E_BLOCKS)]
-        nc.scalar.dma_start(entry_weights[0][:], mask[0:P, 0:PIECE])
+        for piece in range(PIECES):
+            nc.scalar.dma_start(entry_weights[piece][:], mask[0:P, piece * PIECE : (piece + 1) * PIECE])
         nc.scalar.dma_start(w_blocks[:], w.rearrange("(cb p) e -> p cb e", p=P))
         for eb in range(E_BLOCKS):
             nc.scalar.dma_start(biases[eb][:], b[eb * P : (eb + 1) * P, :])
-        nc.scalar.dma_start(entry_weights[1][:], mask[0:P, PIECE : 2 * PIECE])
 
         x_blocks = []
         for cb in range(C_BLOCKS):
-            x_block = windows.tile([P, S], F32, name="x_block")
+            x_block = blocks.tile([P, S], F32, name="x_block")
             nc.sync.dma_start(x_block[:], x[cb * P : (cb + 1) * P, :])
             x_blocks.append(x_block)
 
         identity = held.tile([P, P], F32, name="identity")
         make_identity(nc, identity[:])
-
-        def gather_times_mask(product, cb, piece):
-            nc.vector.tensor_tensor(
-                product,
-                x_blocks[cb][:].indirect(
-                    offsets[:, piece * (PIECE // 16) : (piece + 1) * (PIECE // 16)]
-                ),
-                entry_weights[piece][:],
-                mult,
-            )
-
-        warm_up = psum.tile([P, BANK], F32, name="warm_up")
-        for repeat in range(WARM_UP_MATMULS):
-            nc.tensor.matmul(
-                warm_up[:],
-                w_blocks[:, 0, 0:P],
-                w_blocks[:, 0 : BANK // E, :].rearrange("p cb e -> p (cb e)"),
-                start=True,
-                stop=True,
-            )
+        identity_bf16 = held.tile([P, P], BF16, name="identity_bf16")
+        make_identity(nc, identity_bf16[:])
 
         pooled = held.tile([P, C_BLOCKS, Q], BF16, name="pooled")
-
-        for pair in range(PAIRS):
-            pair_products = held.tile([P, PAIR, PIECE], F32, name=f"pair_products{pair}")
-            for k in range(PAIR):
-                gather_times_mask(pair_products[:, k, :], pair * PAIR + k, 0)
-            by_token = pair_products[:].rearrange("p k (m t) -> p t (k m)", t=T)
-            pooled_f32 = psum_pooled.tile([P, PAIR, PIECE_Q], F32, name="pooled_f32")
-            for t in range(T):
-                nc.tensor.matmul(
-                    pooled_f32[:].rearrange("p k m -> p (k m)"),
-                    identity[:],
-                    by_token[:, t, :],
-                    start=(t == 0),
-                    stop=(t == T - 1),
-                )
-            nc.scalar.activation(
-                pooled[:, pair * PAIR : (pair + 1) * PAIR, 0:PIECE_Q],
-                pooled_f32[:],
-                mybir.ActivationFunctionType.Copy,
-            )
-
         sums = [psum.tile([P, Q], F32, name=f"sums{eb}") for eb in range(E_BLOCKS)]
+
         for cb in range(C_BLOCKS):
-            product = products.tile([P, PIECE], F32, name="product")
-            gather_times_mask(product[:], cb, 1)
-            with nc.allow_low_precision(reason="pooled is rounded once to bfloat16"):
-                nc.vector.tensor_reduce(
-                    pooled[:, cb, PIECE_Q:Q],
-                    product[:].rearrange("p (m t) -> p m t", t=T),
-                    mybir.AxisListType.X,
-                    add,
+            products = blocks.tile([P, N], F32, name="products")
+            for piece in range(PIECES):
+                nc.vector.tensor_tensor(
+                    products[:, piece * PIECE : (piece + 1) * PIECE],
+                    x_blocks[cb][:].indirect(
+                        offsets[:, piece * (PIECE // 16) : (piece + 1) * (PIECE // 16)]
+                    ),
+                    entry_weights[piece][:],
+                    mult,
                 )
+
+            if cb < C_BLOCKS - 1:
+                by_token = products[:].rearrange("p (m t) -> p t m", t=T)
+                sums_by_mention = psum_blocks.tile([Q, P], F32, name="sums_by_mention")
+                for t in range(T):
+                    nc.tensor.matmul(
+                        sums_by_mention[:],
+                        by_token[:, t, :],
+                        identity[:],
+                        is_transpose=True,
+                        start=(t == 0),
+                        stop=(t == T - 1),
+                    )
+                pooled_by_mention = blocks.tile([Q, P], BF16, name="pooled_by_mention")
+                nc.scalar.activation(pooled_by_mention[:], sums_by_mention[:], copy)
+                pooled_back = psum_blocks.tile([P, Q], BF16, name="pooled_back")
+                nc.tensor.transpose(pooled_back[:], pooled_by_mention[:], identity_bf16[:])
+                nc.scalar.activation(pooled[:, cb, :], pooled_back[:], copy)
+            else:
+                with nc.allow_low_precision(reason="pooled is rounded once to bfloat16"):
+                    nc.vector.tensor_reduce(
+                        pooled[:, cb, :],
+                        products[:].rearrange("p (m t) -> p m t", t=T),
+                        mybir.AxisListType.X,
+                        add,
+                    )
+
             for eb in range(E_BLOCKS):
                 nc.tensor.matmul(
                     sums[eb][:],
@@ -114,7 +100,5 @@ def tile_graphstatelstm_kernel(tc, x, mask, w, b, offs, out):
 
         for eb in range(E_BLOCKS):
             result = results.tile([P, Q], F32, name="result")
-            nc.scalar.activation(
-                result[:], sums[eb][:], mybir.ActivationFunctionType.Tanh, bias=biases[eb][:]
-            )
+            nc.scalar.activation(result[:], sums[eb][:], tanh, bias=biases[eb][:])
             nc.sync.dma_start(out[eb * P : (eb + 1) * P, :], result[:])

@@ -9,6 +9,9 @@ C_BLOCKS = C // P
 E_BLOCKS = E // P
 PIECE = S
 PIECES = N // PIECE
+PIECE_Q = PIECE // T
+HALVES = P // PIECE_Q
+HALF_T = T // HALVES
 
 FLOPS = 2 * C * N + 2 * C * E * Q
 BYTES = 4 * C * S + 4 * N + 2 * C * E + 4 * E + 2 * P * (N // 16) + 4 * E * Q
@@ -21,9 +24,10 @@ def tile_graphstatelstm_kernel(tc, x, mask, w, b, offs, out):
     with (
         tc.tile_pool(name="held", bufs=1) as held,
         tc.tile_pool(name="blocks", bufs=C_BLOCKS) as blocks,
+        tc.tile_pool(name="pieces", bufs=3) as pieces,
         tc.tile_pool(name="results", bufs=E_BLOCKS) as results,
         tc.psum_pool(name="psum", bufs=1) as psum,
-        tc.psum_pool(name="psum_blocks", bufs=2) as psum_blocks,
+        tc.psum_pool(name="psum_pieces", bufs=2) as psum_pieces,
     ):
         offsets = held.tile([P, N // 16], U16, name="offsets")
         nc.sync.dma_start(offsets[:], offs)
@@ -45,49 +49,55 @@ def tile_graphstatelstm_kernel(tc, x, mask, w, b, offs, out):
 
         identity = held.tile([P, P], F32, name="identity")
         make_identity(nc, identity[:])
-        identity_bf16 = held.tile([P, P], BF16, name="identity_bf16")
-        make_identity(nc, identity_bf16[:])
+        half_adder = held.tile([P, PIECE_Q], F32, name="half_adder")
+        nc.vector.tensor_reduce(
+            half_adder[:],
+            identity[:].rearrange("p (m h) -> p m h", h=HALVES),
+            mybir.AxisListType.X,
+            add,
+        )
 
         pooled = held.tile([P, C_BLOCKS, Q], BF16, name="pooled")
         sums = [psum.tile([P, Q], F32, name=f"sums{eb}") for eb in range(E_BLOCKS)]
 
         for cb in range(C_BLOCKS):
-            products = blocks.tile([P, N], F32, name="products")
             for piece in range(PIECES):
+                products = pieces.tile([P, PIECE], F32, name="products")
                 nc.vector.tensor_tensor(
-                    products[:, piece * PIECE : (piece + 1) * PIECE],
+                    products[:],
                     x_blocks[cb][:].indirect(
                         offsets[:, piece * (PIECE // 16) : (piece + 1) * (PIECE // 16)]
                     ),
                     entry_weights[piece][:],
                     mult,
                 )
+                pooled_piece = pooled[:, cb, piece * PIECE_Q : (piece + 1) * PIECE_Q]
 
-            if cb < C_BLOCKS - 1:
-                by_token = products[:].rearrange("p (m t) -> p t m", t=T)
-                sums_by_mention = psum_blocks.tile([Q, P], F32, name="sums_by_mention")
-                for t in range(T):
-                    nc.tensor.matmul(
-                        sums_by_mention[:],
-                        by_token[:, t, :],
-                        identity[:],
-                        is_transpose=True,
-                        start=(t == 0),
-                        stop=(t == T - 1),
-                    )
-                pooled_by_mention = blocks.tile([Q, P], BF16, name="pooled_by_mention")
-                nc.scalar.activation(pooled_by_mention[:], sums_by_mention[:], copy)
-                pooled_back = psum_blocks.tile([P, Q], BF16, name="pooled_back")
-                nc.tensor.transpose(pooled_back[:], pooled_by_mention[:], identity_bf16[:])
-                nc.scalar.activation(pooled[:, cb, :], pooled_back[:], copy)
-            else:
-                with nc.allow_low_precision(reason="pooled is rounded once to bfloat16"):
-                    nc.vector.tensor_reduce(
-                        pooled[:, cb, :],
-                        products[:].rearrange("p (m t) -> p m t", t=T),
-                        mybir.AxisListType.X,
-                        add,
-                    )
+                if (cb, piece) == (C_BLOCKS - 1, PIECES - 1):
+                    with nc.allow_low_precision(reason="pooled is rounded once to bfloat16"):
+                        nc.vector.tensor_reduce(
+                            pooled_piece,
+                            products[:].rearrange("p (m t) -> p m t", t=T),
+                            mybir.AxisListType.X,
+                            add,
+                        )
+                else:
+                    by_token = products[:].rearrange("p (k u) -> p u k", u=HALF_T)
+                    half_sums_psum = psum_pieces.tile([P, P], F32, name="half_sums_psum")
+                    for u in range(HALF_T):
+                        nc.tensor.matmul(
+                            half_sums_psum[:],
+                            by_token[:, u, :],
+                            identity[:],
+                            is_transpose=True,
+                            start=(u == 0),
+                            stop=(u == HALF_T - 1),
+                        )
+                    half_sums = pieces.tile([P, P], F32, name="half_sums")
+                    nc.scalar.activation(half_sums[:], half_sums_psum[:], copy)
+                    pooled_psum = psum_pieces.tile([P, PIECE_Q], F32, name="pooled_psum")
+                    nc.tensor.matmul(pooled_psum[:], half_sums[:], half_adder[:], start=True, stop=True)
+                    nc.scalar.activation(pooled_piece, pooled_psum[:], copy)
 
             for eb in range(E_BLOCKS):
                 nc.tensor.matmul(

@@ -10,6 +10,7 @@ E_BLOCKS = E // P
 PIECE = S
 PIECES = N // PIECE
 PIECE_Q = PIECE // T
+FIRST = PIECE // 4
 HALVES = P // PIECE_Q
 HALF_T = T // HALVES
 
@@ -23,7 +24,6 @@ def tile_graphstatelstm_kernel(tc, x, mask, w, b, offs, out):
     copy, tanh = mybir.ActivationFunctionType.Copy, mybir.ActivationFunctionType.Tanh
     with (
         tc.tile_pool(name="held", bufs=1) as held,
-        tc.tile_pool(name="blocks", bufs=C_BLOCKS) as blocks,
         tc.tile_pool(name="pieces", bufs=3) as pieces,
         tc.tile_pool(name="results", bufs=E_BLOCKS) as results,
         tc.psum_pool(name="psum", bufs=1) as psum,
@@ -32,30 +32,32 @@ def tile_graphstatelstm_kernel(tc, x, mask, w, b, offs, out):
         offsets = held.tile([P, N // 16], U16, name="offsets")
         nc.sync.dma_start(offsets[:], offs)
 
+        def load_in_halves(tile_columns, dram_columns):
+            half = tile_columns.shape[1] // 2
+            nc.sync.dma_start(tile_columns[:, :half], dram_columns[:, :half])
+            nc.scalar.dma_start(tile_columns[:, half:], dram_columns[:, half:])
+
         entry_weights = [held.tile([P, PIECE], F32, name=f"entry_weights{piece}") for piece in range(PIECES)]
+        x_blocks = [held.tile([P, S], F32, name=f"x_block{cb}") for cb in range(C_BLOCKS)]
         w_blocks = held.tile([P, C_BLOCKS, E], BF16, name="w_blocks")
         biases = [held.tile([P, 1], F32, name=f"bias{eb}") for eb in range(E_BLOCKS)]
-        for piece in range(PIECES):
-            nc.scalar.dma_start(entry_weights[piece][:], mask[0:P, piece * PIECE : (piece + 1) * PIECE])
-        nc.scalar.dma_start(w_blocks[:], w.rearrange("(cb p) e -> p cb e", p=P))
+
+        load_in_halves(x_blocks[0][:], x[0:P, :])
+        load_in_halves(entry_weights[0][:, :FIRST], mask[0:P, :FIRST])
+        load_in_halves(entry_weights[0][:, FIRST:], mask[0:P, FIRST:PIECE])
+        load_in_halves(entry_weights[1][:], mask[0:P, PIECE : 2 * PIECE])
+        load_in_halves(x_blocks[1][:], x[P : 2 * P, :])
+        load_in_halves(w_blocks[:], w.rearrange("(cb p) e -> p cb e", p=P))
+        for cb in range(2, C_BLOCKS):
+            load_in_halves(x_blocks[cb][:], x[cb * P : (cb + 1) * P, :])
         for eb in range(E_BLOCKS):
             nc.scalar.dma_start(biases[eb][:], b[eb * P : (eb + 1) * P, :])
-
-        x_blocks = []
-        for cb in range(C_BLOCKS):
-            x_block = blocks.tile([P, S], F32, name="x_block")
-            nc.sync.dma_start(x_block[:], x[cb * P : (cb + 1) * P, :])
-            x_blocks.append(x_block)
 
         identity = held.tile([P, P], F32, name="identity")
         make_identity(nc, identity[:])
         half_adder = held.tile([P, PIECE_Q], F32, name="half_adder")
-        nc.vector.tensor_reduce(
-            half_adder[:],
-            identity[:].rearrange("p (m h) -> p m h", h=HALVES),
-            mybir.AxisListType.X,
-            add,
-        )
+        identity_halves = identity[:].rearrange("p (m h) -> p h m", h=HALVES)
+        nc.gpsimd.tensor_tensor(half_adder[:], identity_halves[:, 0, :], identity_halves[:, 1, :], add)
 
         pooled = held.tile([P, C_BLOCKS, Q], BF16, name="pooled")
         sums = [psum.tile([P, Q], F32, name=f"sums{eb}") for eb in range(E_BLOCKS)]
@@ -63,14 +65,16 @@ def tile_graphstatelstm_kernel(tc, x, mask, w, b, offs, out):
         for cb in range(C_BLOCKS):
             for piece in range(PIECES):
                 products = pieces.tile([P, PIECE], F32, name="products")
-                nc.vector.tensor_tensor(
-                    products[:],
-                    x_blocks[cb][:].indirect(
-                        offsets[:, piece * (PIECE // 16) : (piece + 1) * (PIECE // 16)]
-                    ),
-                    entry_weights[piece][:],
-                    mult,
-                )
+                cuts = (0, FIRST, PIECE) if (cb, piece) == (0, 0) else (0, PIECE)
+                for lo, hi in zip(cuts[:-1], cuts[1:]):
+                    nc.vector.tensor_tensor(
+                        products[:, lo:hi],
+                        x_blocks[cb][:].indirect(
+                            offsets[:, (piece * PIECE + lo) // 16 : (piece * PIECE + hi) // 16]
+                        ),
+                        entry_weights[piece][:, lo:hi],
+                        mult,
+                    )
                 pooled_piece = pooled[:, cb, piece * PIECE_Q : (piece + 1) * PIECE_Q]
 
                 if (cb, piece) == (C_BLOCKS - 1, PIECES - 1):

@@ -25,7 +25,7 @@ def tile_graphstatelstm_kernel(tc, x, mask, w, b, offs, out):
     with (
         tc.tile_pool(name="held", bufs=1) as held,
         tc.tile_pool(name="pieces", bufs=3) as pieces,
-        tc.tile_pool(name="results", bufs=E_BLOCKS) as results,
+        tc.tile_pool(name="results", bufs=PIECES * E_BLOCKS) as results,
         tc.psum_pool(name="psum", bufs=1) as psum,
         tc.psum_pool(name="psum_pieces", bufs=2) as psum_pieces,
     ):
@@ -45,11 +45,10 @@ def tile_graphstatelstm_kernel(tc, x, mask, w, b, offs, out):
         load_in_halves(x_blocks[0][:], x[0:P, :])
         load_in_halves(entry_weights[0][:, :FIRST], mask[0:P, :FIRST])
         load_in_halves(entry_weights[0][:, FIRST:], mask[0:P, FIRST:PIECE])
-        load_in_halves(entry_weights[1][:], mask[0:P, PIECE : 2 * PIECE])
-        load_in_halves(x_blocks[1][:], x[P : 2 * P, :])
-        load_in_halves(w_blocks[:], w.rearrange("(cb p) e -> p cb e", p=P))
-        for cb in range(2, C_BLOCKS):
+        for cb in range(1, C_BLOCKS):
             load_in_halves(x_blocks[cb][:], x[cb * P : (cb + 1) * P, :])
+        load_in_halves(w_blocks[:], w.rearrange("(cb p) e -> p cb e", p=P))
+        load_in_halves(entry_weights[1][:], mask[0:P, PIECE : 2 * PIECE])
         for eb in range(E_BLOCKS):
             nc.scalar.dma_start(biases[eb][:], b[eb * P : (eb + 1) * P, :])
 
@@ -60,10 +59,13 @@ def tile_graphstatelstm_kernel(tc, x, mask, w, b, offs, out):
         nc.gpsimd.tensor_tensor(half_adder[:], identity_halves[:, 0, :], identity_halves[:, 1, :], add)
 
         pooled = held.tile([P, C_BLOCKS, Q], BF16, name="pooled")
-        sums = [psum.tile([P, Q], F32, name=f"sums{eb}") for eb in range(E_BLOCKS)]
+        sums = [
+            [psum.tile([P, PIECE_Q], F32, name=f"sums{piece}{eb}") for eb in range(E_BLOCKS)]
+            for piece in range(PIECES)
+        ]
 
-        for cb in range(C_BLOCKS):
-            for piece in range(PIECES):
+        for piece in range(PIECES):
+            for cb in range(C_BLOCKS):
                 products = pieces.tile([P, PIECE], F32, name="products")
                 cuts = (0, FIRST, PIECE) if (cb, piece) == (0, 0) else (0, PIECE)
                 for lo, hi in zip(cuts[:-1], cuts[1:]):
@@ -103,16 +105,20 @@ def tile_graphstatelstm_kernel(tc, x, mask, w, b, offs, out):
                     nc.tensor.matmul(pooled_psum[:], half_sums[:], half_adder[:], start=True, stop=True)
                     nc.scalar.activation(pooled_piece, pooled_psum[:], copy)
 
-            for eb in range(E_BLOCKS):
-                nc.tensor.matmul(
-                    sums[eb][:],
-                    w_blocks[:, cb, eb * P : (eb + 1) * P],
-                    pooled[:, cb, :],
-                    start=(cb == 0),
-                    stop=(cb == C_BLOCKS - 1),
-                )
-
-        for eb in range(E_BLOCKS):
-            result = results.tile([P, Q], F32, name="result")
-            nc.scalar.activation(result[:], sums[eb][:], tanh, bias=biases[eb][:])
-            nc.sync.dma_start(out[eb * P : (eb + 1) * P, :], result[:])
+                for eb in range(E_BLOCKS):
+                    nc.tensor.matmul(
+                        sums[piece][eb][:],
+                        w_blocks[:, cb, eb * P : (eb + 1) * P],
+                        pooled_piece,
+                        start=(cb == 0),
+                        stop=(cb == C_BLOCKS - 1),
+                    )
+                if cb == C_BLOCKS - 1:
+                    for eb in range(E_BLOCKS):
+                        result = results.tile([P, PIECE_Q], F32, name="result")
+                        nc.scalar.activation(result[:], sums[piece][eb][:], tanh, bias=biases[eb][:])
+                        last = (piece, eb) == (PIECES - 1, E_BLOCKS - 1)
+                        store_queue = nc.scalar if last else nc.sync
+                        store_queue.dma_start(
+                            out[eb * P : (eb + 1) * P, piece * PIECE_Q : (piece + 1) * PIECE_Q], result[:]
+                        )

@@ -10,7 +10,7 @@ E_BLOCKS = E // P
 PIECE = S
 PIECES = N // PIECE
 PIECE_Q = PIECE // T
-FIRST = PIECE // 4
+FIRST = PIECE // 2
 HALVES = P // PIECE_Q
 HALF_T = T // HALVES
 

@@ -32,25 +32,20 @@ def tile_graphstatelstm_kernel(tc, x, mask, w, b, offs, out):
         offsets = held.tile([P, N // 16], U16, name="offsets")
         nc.sync.dma_start(offsets[:], offs)
 
-        def load_in_halves(tile_columns, dram_columns):
-            half = tile_columns.shape[1] // 2
-            nc.sync.dma_start(tile_columns[:, :half], dram_columns[:, :half])
-            nc.scalar.dma_start(tile_columns[:, half:], dram_columns[:, half:])
-
         entry_weights = [held.tile([P, PIECE], F32, name=f"entry_weights{piece}") for piece in range(PIECES)]
         x_blocks = [held.tile([P, S], F32, name=f"x_block{cb}") for cb in range(C_BLOCKS)]
         w_blocks = held.tile([P, C_BLOCKS, E], BF16, name="w_blocks")
         biases = [held.tile([P, 1], F32, name=f"bias{eb}") for eb in range(E_BLOCKS)]
 
-        load_in_halves(x_blocks[0][:], x[0:P, :])
-        load_in_halves(entry_weights[0][:, :FIRST], mask[0:P, :FIRST])
-        load_in_halves(entry_weights[0][:, FIRST:], mask[0:P, FIRST:PIECE])
+        nc.sync.dma_start(x_blocks[0][:], x[0:P, :])
+        nc.sync.dma_start(entry_weights[0][:, :FIRST], mask[0:P, :FIRST])
+        nc.sync.dma_start(entry_weights[0][:, FIRST:], mask[0:P, FIRST:PIECE])
         for cb in range(1, C_BLOCKS):
-            load_in_halves(x_blocks[cb][:], x[cb * P : (cb + 1) * P, :])
-        load_in_halves(w_blocks[:], w.rearrange("(cb p) e -> p cb e", p=P))
-        load_in_halves(entry_weights[1][:], mask[0:P, PIECE : 2 * PIECE])
+            nc.sync.dma_start(x_blocks[cb][:], x[cb * P : (cb + 1) * P, :])
+        nc.sync.dma_start(w_blocks[:], w.rearrange("(cb p) e -> p cb e", p=P))
+        nc.sync.dma_start(entry_weights[1][:], mask[0:P, PIECE : 2 * PIECE])
         for eb in range(E_BLOCKS):
-            nc.scalar.dma_start(biases[eb][:], b[eb * P : (eb + 1) * P, :])
+            nc.sync.dma_start(biases[eb][:], b[eb * P : (eb + 1) * P, :])
 
         identity = held.tile([P, P], F32, name="identity")
         make_identity(nc, identity[:])

@@ -10,7 +10,7 @@ E_BLOCKS = E // P
 PIECE = S
 PIECES = N // PIECE
 PIECE_Q = PIECE // T
-FIRST = PIECE // 2
+FIRST = 3 * PIECE // 8
 HALVES = P // PIECE_Q
 HALF_T = T // HALVES
 

import concourse.mybir as mybir
from concourse.masks import make_identity

F32, BF16, U16 = mybir.dt.float32, mybir.dt.bfloat16, mybir.dt.uint16

P = 128
C, S, N, T, Q, E = 512, 1024, 2048, 16, 128, 256
C_BLOCKS = C // P
E_BLOCKS = E // P
PIECE = S
PIECES = N // PIECE
PIECE_Q = PIECE // T
FIRST = 3 * PIECE // 8
HALVES = P // PIECE_Q
HALF_T = T // HALVES

FLOPS = 2 * C * N + 2 * C * E * Q
BYTES = 4 * C * S + 4 * N + 2 * C * E + 4 * E + 2 * P * (N // 16) + 4 * E * Q


def tile_graphstatelstm_kernel(tc, x, mask, w, b, offs, out):
    nc = tc.nc
    mult, add = mybir.AluOpType.mult, mybir.AluOpType.add
    copy, tanh = mybir.ActivationFunctionType.Copy, mybir.ActivationFunctionType.Tanh
    with (
        tc.tile_pool(name="held", bufs=1) as held,
        tc.tile_pool(name="pieces", bufs=3) as pieces,
        tc.tile_pool(name="results", bufs=PIECES * E_BLOCKS) as results,
        tc.psum_pool(name="psum", bufs=1) as psum,
        tc.psum_pool(name="psum_pieces", bufs=2) as psum_pieces,
    ):
        offsets = held.tile([P, N // 16], U16, name="offsets")
        nc.sync.dma_start(offsets[:], offs)

        entry_weights = [held.tile([P, PIECE], F32, name=f"entry_weights{piece}") for piece in range(PIECES)]
        x_blocks = [held.tile([P, S], F32, name=f"x_block{cb}") for cb in range(C_BLOCKS)]
        w_blocks = held.tile([P, C_BLOCKS, E], BF16, name="w_blocks")
        biases = [held.tile([P, 1], F32, name=f"bias{eb}") for eb in range(E_BLOCKS)]

        nc.sync.dma_start(x_blocks[0][:], x[0:P, :])
        nc.sync.dma_start(entry_weights[0][:, :FIRST], mask[0:P, :FIRST])
        nc.sync.dma_start(entry_weights[0][:, FIRST:], mask[0:P, FIRST:PIECE])
        for cb in range(1, C_BLOCKS):
            nc.sync.dma_start(x_blocks[cb][:], x[cb * P : (cb + 1) * P, :])
        nc.sync.dma_start(w_blocks[:], w.rearrange("(cb p) e -> p cb e", p=P))
        nc.sync.dma_start(entry_weights[1][:], mask[0:P, PIECE : 2 * PIECE])
        for eb in range(E_BLOCKS):
            nc.sync.dma_start(biases[eb][:], b[eb * P : (eb + 1) * P, :])

        identity = held.tile([P, P], F32, name="identity")
        make_identity(nc, identity[:])
        half_adder = held.tile([P, PIECE_Q], F32, name="half_adder")
        identity_halves = identity[:].rearrange("p (m h) -> p h m", h=HALVES)
        nc.gpsimd.tensor_tensor(half_adder[:], identity_halves[:, 0, :], identity_halves[:, 1, :], add)

        pooled = held.tile([P, C_BLOCKS, Q], BF16, name="pooled")
        sums = [
            [psum.tile([P, PIECE_Q], F32, name=f"sums{piece}{eb}") for eb in range(E_BLOCKS)]
            for piece in range(PIECES)
        ]

        for piece in range(PIECES):
            for cb in range(C_BLOCKS):
                products = pieces.tile([P, PIECE], F32, name="products")
                cuts = (0, FIRST, PIECE) if (cb, piece) == (0, 0) else (0, PIECE)
                for lo, hi in zip(cuts[:-1], cuts[1:]):
                    nc.vector.tensor_tensor(
                        products[:, lo:hi],
                        x_blocks[cb][:].indirect(
                            offsets[:, (piece * PIECE + lo) // 16 : (piece * PIECE + hi) // 16]
                        ),
                        entry_weights[piece][:, lo:hi],
                        mult,
                    )
                pooled_piece = pooled[:, cb, piece * PIECE_Q : (piece + 1) * PIECE_Q]

                if (cb, piece) == (C_BLOCKS - 1, PIECES - 1):
                    with nc.allow_low_precision(reason="pooled is rounded once to bfloat16"):
                        nc.vector.tensor_reduce(
                            pooled_piece,
                            products[:].rearrange("p (m t) -> p m t", t=T),
                            mybir.AxisListType.X,
                            add,
                        )
                else:
                    by_token = products[:].rearrange("p (k u) -> p u k", u=HALF_T)
                    half_sums_psum = psum_pieces.tile([P, P], F32, name="half_sums_psum")
                    for u in range(HALF_T):
                        nc.tensor.matmul(
                            half_sums_psum[:],
                            by_token[:, u, :],
                            identity[:],
                            is_transpose=True,
                            start=(u == 0),
                            stop=(u == HALF_T - 1),
                        )
                    half_sums = pieces.tile([P, P], F32, name="half_sums")
                    nc.scalar.activation(half_sums[:], half_sums_psum[:], copy)
                    pooled_psum = psum_pieces.tile([P, PIECE_Q], F32, name="pooled_psum")
                    nc.tensor.matmul(pooled_psum[:], half_sums[:], half_adder[:], start=True, stop=True)
                    nc.scalar.activation(pooled_piece, pooled_psum[:], copy)

                for eb in range(E_BLOCKS):
                    nc.tensor.matmul(
                        sums[piece][eb][:],
                        w_blocks[:, cb, eb * P : (eb + 1) * P],
                        pooled_piece,
                        start=(cb == 0),
                        stop=(cb == C_BLOCKS - 1),
                    )
                if cb == C_BLOCKS - 1:
                    for eb in range(E_BLOCKS):
                        result = results.tile([P, PIECE_Q], F32, name="result")
                        nc.scalar.activation(result[:], sums[piece][eb][:], tanh, bias=biases[eb][:])
                        last = (piece, eb) == (PIECES - 1, E_BLOCKS - 1)
                        store_queue = nc.scalar if last else nc.sync
                        store_queue.dma_start(
                            out[eb * P : (eb + 1) * P, piece * PIECE_Q : (piece + 1) * PIECE_Q], result[:]
                        )
